import numpy as np
import ml_dtypes


def mxq(x, axis, fmt="e4m3"):
    dtype, down = {"e4m3": (ml_dtypes.float8_e4m3fn, 7), "e5m2": (ml_dtypes.float8_e5m2, 14)}[fmt]
    v = np.moveaxis(np.asarray(x, np.float32).astype(ml_dtypes.bfloat16).astype(np.float64), axis, -1)
    blocks = v.reshape(v.shape[:-1] + (-1, 32))
    amax = np.abs(blocks).max(-1, keepdims=True)
    byte = np.maximum(np.where(amax > 0, np.frexp(amax)[1] - 1 + 127, 0) - down, 1)
    scale = np.exp2(byte - 127.0)
    codes = (blocks / scale).astype(np.float32).astype(dtype).astype(np.float64)
    return np.moveaxis((codes * scale).reshape(v.shape), -1, axis)


WIDE = False


def mx_kscale(k):
    if not WIDE:
        return np.ones(k)
    levels = np.array([10, -10, 5, -5, 0])
    if k % 512:
        return np.exp2(np.random.permutation(np.resize(levels, k // 32))).repeat(32)
    a = np.empty((k // 512, 16))
    for p in range(k // 512):
        a[p, :8] = np.random.permutation(np.resize(levels, 8))
        for g in range(8):
            far = levels[np.abs(levels - a[p, g]) >= 10]
            a[p, g + 8] = far[np.random.randint(len(far))]
    return np.exp2(a.ravel()).repeat(32)


BF16 = ml_dtypes.bfloat16


def bf(x):
    return np.asarray(x, np.float32).astype(BF16)


def f64(x):
    return np.asarray(x).astype(np.float64)


N, IN_F, OUT_F = 1024, 512, 512
POW = 2


def setup_inputs():
    s = mx_kscale(IN_F)
    u = np.exp2(np.round(np.log2(mx_kscale(N)) / 2))
    return {"input": bf(np.random.standard_normal((N, IN_F)) * s / (u * u)[:, None]),
            "adj": bf(np.random.uniform(0.0, 1.0, (N, N)) * 1.5 / N ** 0.25 * u),
            "weight": bf(np.random.uniform(-1.0, 1.0, (IN_F, OUT_F)) * 1.7 / np.sqrt(IN_F) / s[:, None]),
            "bias": bf(np.random.standard_normal(OUT_F) * 0.3)}


def reference(input, adj, weight, bias):
    k_adj = f64(adj) ** POW
    support = mxq(f64(input), 1, "e4m3") @ mxq(f64(weight), 0, "e4m3")
    out = (mxq(k_adj, 1, "e4m3") @ mxq(support, 0, "e4m3")) + f64(bias)
    return np.where(out > 0, out, np.expm1(out))

@@ -1,0 +1,273 @@
+from contextlib import ExitStack
+
+import concourse.mybir as mybir
+from concourse.masks import make_identity
+
+FLOPS = 2 * 1024 * 512 * 512 + 2 * 1024 * 1024 * 512
+
+F32 = mybir.dt.float32
+BF16 = mybir.dt.bfloat16
+U32 = mybir.dt.uint32
+U8 = mybir.dt.uint8
+FP8X4 = mybir.dt.float8_e4m3fn_x4
+ALU = mybir.AluOpType
+ACT = mybir.ActivationFunctionType
+
+P = 128
+NODES = 1024
+FEAT = 512
+OUTF = 512
+MANUAL = True
+AHEAD = 3
+NWARM = 6
+MIN_ON_SCALAR = (5, 6)
+SPLIT_TILES = (7,)
+SC_ON_VECTOR = (1, 3)
+BANK_DT = F32
+
+
+def tile_netgraphconvolution_kernel(tc, x, adj, weight, bias, out):
+    nc = tc.nc
+    with ExitStack() as ctx:
+        keep = ctx.enter_context(tc.tile_pool(name="keep", bufs=1))
+        psum = ctx.enter_context(tc.psum_pool(name="psum", bufs=8))
+        if MANUAL:
+            ctx.enter_context(tc.manual_schedule())
+
+        bias_row = keep.tile([P, OUTF], BF16, name="bias_row", tag="bias_row")
+        ones = keep.tile([P, P], BF16, name="ones", tag="ones")
+        warm = keep.tile([P, 8], F32, name="warm", tag="warm")
+        zeros = keep.tile([P, OUTF], BF16, name="zeros", tag="zeros")
+        nc.vector.memset(warm[:], 0.0)
+        nc.vector.memset(ones[:], 1.0)
+        nc.vector.memset(zeros[:], 0.0)
+        nc.vector.memset(bias_row[:], 0.0)
+        nc.scalar.activation(out=warm[:, 4:8], in_=warm[:, 0:4], func=ACT.Exp)
+        nc.scalar.dma_start(out=bias_row[0:1, :], in_=bias.rearrange("(a o) -> a o", a=1))
+
+        w_raw = keep.tile([P, 4, OUTF], BF16, name="w_raw", tag="w_raw")
+        nc.sync.dma_start(out=w_raw[:], in_=weight.rearrange("(p j) o -> p j o", j=4))
+        x_view = x.rearrange("(u m s) f -> u m s f", m=P, s=4)
+        x_raw = []
+        for u in range(4):
+            t = keep.tile([P, 2, FEAT], BF16, name="x_raw%d" % u, tag="x_raw%d" % u)
+            g, h = divmod(u, 2)
+            nc.sync.dma_start(out=t[:], in_=x_view[g, :, 2 * h : 2 * h + 2, :])
+            x_raw.append(t)
+        a_raw = []
+        for i in range(8):
+            t = keep.tile([P, NODES], BF16, name="a_raw%d" % i, tag="a_raw%d" % i)
+            nc.sync.dma_start(out=t[:], in_=adj[i * P : (i + 1) * P, :])
+            a_raw.append(t)
+
+        ident = keep.tile([P, P], F32, name="ident", tag="ident")
+        make_identity(nc, ident[:])
+        bank_w = psum.tile([P, OUTF], F32, name="bank_w", tag="bank")
+        for n in range(NWARM):
+            nc.tensor.matmul(out=bank_w[:], lhsT=ones[:], rhs=zeros[:], start=True, stop=True)
+
+        w_grp = keep.tile([P, OUTF, 4], BF16, name="w_grp", tag="w_grp", align_bytes=64)
+        w_codes = keep.tile([P, OUTF], U32, name="w_codes", tag="w_codes", align_bytes=64)
+        w_scales = keep.tile([P, OUTF], U8, name="w_scales", tag="w_scales", align_bytes=64)
+        HALF = OUTF // 2
+        for c in range(2):
+            cols = slice(c * HALF, (c + 1) * HALF)
+            nc.vector.tensor_copy(out=w_grp[:, cols, :], in_=w_raw[:, :, cols].rearrange("p j o -> p o j"))
+        for c in range(2):
+            cols = slice(c * HALF, (c + 1) * HALF)
+            nc.vector.quantize_mx(
+                out=w_codes[:, cols].bitcast(FP8X4),
+                scales=w_scales[:, cols],
+                in_=w_grp[:, cols, :].rearrange("p o j -> p (o j)"),
+            )
+
+        x_codes = []
+        x_scales = []
+        x_grp = []
+
+        def x_turn(u):
+            bank = psum.tile([P, 512], F32, name="bank_x%d" % u, tag="bank")
+            for s in range(2):
+                words = x_raw[u][:, s, :].bitcast(F32)
+                for e in range(2):
+                    c0 = e * 256 + s * P
+                    nc.tensor.transpose(out=bank[:, c0 : c0 + P], in_=words[:, e:256:2], identity=ident[:])
+            grp = keep.tile([P, 1024], BF16, name="x_grp%d" % u, tag="x_grp%d" % u, align_bytes=64)
+            nc.scalar.copy(
+                out=grp[:].bitcast(F32).rearrange("p (q e) -> p q e", e=2),
+                in_=bank[:].rearrange("p (e q) -> p q e", e=2),
+            )
+            x_grp.append(grp)
+
+        def x_quant(u):
+            codes = keep.tile([P, 256], U32, name="x_codes%d" % u, tag="x_codes%d" % u, align_bytes=64)
+            scales = keep.tile([P, 256], U8, name="x_scales%d" % u, tag="x_scales%d" % u, align_bytes=64)
+            nc.vector.quantize_mx(out=codes[:].bitcast(FP8X4), scales=scales[:], in_=x_grp[u][:])
+            x_codes.append(codes)
+            x_scales.append(scales)
+
+        for u in range(4):
+            x_turn(u)
+            x_quant(u)
+
+
+        k_grp = {}
+        k_codes = {}
+        k_scales = {}
+
+        def a_turn(i):
+            bank = psum.tile([P, 512], F32, name="bank_a%d" % i, tag="bank")
+            words = a_raw[i][:].bitcast(F32)
+            for g in range(2):
+                for e in range(2):
+                    c0 = e * 256 + g * P
+                    nc.tensor.transpose(
+                        out=bank[:, c0 : c0 + P], in_=words[:, 256 * g + e : 256 * (g + 1) : 2], identity=ident[:]
+                    )
+            return bank
+
+        def a_square(i, bank):
+            grp = keep.tile([P, 1024], BF16, name="k_grp%d" % i, tag="k_grp%d" % i, align_bytes=64)
+            nc.scalar.activation(
+                out=grp[:].rearrange("p (q e c) -> p q e c", e=2, c=2),
+                in_=bank[:].bitcast(BF16).rearrange("p (e q c) -> p q e c", e=2, c=2),
+                func=ACT.Square,
+            )
+            k_grp[i] = grp
+
+        def a_quant(i):
+            codes = keep.tile([P, 256], U32, name="k_codes%d" % i, tag="k_codes%d" % i, align_bytes=64)
+            scales = keep.tile([P, 256], U8, name="k_scales%d" % i, tag="k_scales%d" % i, align_bytes=64)
+            nc.vector.quantize_mx(out=codes[:].bitcast(FP8X4), scales=scales[:], in_=k_grp[i][:])
+            k_codes[i] = codes
+            k_scales[i] = scales
+
+        s_raw = []
+        for g in range(2):
+            s_raw_g = keep.tile([P, 4, OUTF], BF16, name="s_raw%d" % g, tag="s_raw%d" % g)
+            s_raw.append(s_raw_g)
+        for k in range(8):
+            u, s = divmod(k, 2)
+            g, t = divmod(k, 4)
+            bank = psum.tile([P, OUTF], BANK_DT, name="bank_s%d" % k, tag="bank")
+            nc.tensor.matmul_mx(
+                out=bank[:],
+                lhsT=x_codes[u][:, s * P : (s + 1) * P].bitcast(FP8X4),
+                lhsT_scale=x_scales[u][:, s * P : (s + 1) * P],
+                rhs=w_codes[:].bitcast(FP8X4),
+                rhs_scale=w_scales[:],
+                start=True,
+                stop=True,
+            )
+            if k in SC_ON_VECTOR:
+                nc.vector.tensor_copy(out=s_raw[g][:, t, :], in_=bank[:])
+            else:
+                nc.scalar.copy(out=s_raw[g][:, t, :], in_=bank[:])
+
+        banks_a = {}
+        for i in range(AHEAD):
+            a_square(i, a_turn(i))
+        banks_a[AHEAD] = a_turn(AHEAD)
+        bank_b = psum.tile([P, OUTF], F32, name="bank_b", tag="bank")
+        nc.tensor.matmul(out=bank_b[:], lhsT=ones[:], rhs=bias_row[:], start=True, stop=True)
+        b1 = keep.tile([P, OUTF], F32, name="b1", tag="b1")
+
+        s_codes = []
+        s_scales = []
+        for g in range(2):
+            grp = keep.tile([P, OUTF, 4], BF16, name="s_grp%d" % g, tag="s_grp%d" % g, align_bytes=64)
+            codes = keep.tile([P, OUTF], U32, name="s_codes%d" % g, tag="s_codes%d" % g, align_bytes=64)
+            scales = keep.tile([P, OUTF], U8, name="s_scales%d" % g, tag="s_scales%d" % g, align_bytes=64)
+            for c in range(2):
+                cols = slice(c * HALF, (c + 1) * HALF)
+                nc.vector.tensor_copy(out=grp[:, cols, :], in_=s_raw[g][:, :, cols].rearrange("p t o -> p o t"))
+            if g == 1:
+                a_quant(0)
+            for c in range(2):
+                cols = slice(c * HALF, (c + 1) * HALF)
+                nc.vector.quantize_mx(
+                    out=codes[:, cols].bitcast(FP8X4),
+                    scales=scales[:, cols],
+                    in_=grp[:, cols, :].rearrange("p o t -> p (o t)"),
+                )
+            s_codes.append(codes)
+            s_scales.append(scales)
+
+        accs = {}
+        vps = {}
+        negs = {}
+        exps = {}
+
+        def pieces(i):
+            if i in SPLIT_TILES:
+                return [slice(0, HALF), slice(HALF, OUTF)]
+            return [slice(0, OUTF)]
+
+        def multiply(i):
+            acc = psum.tile([P, OUTF], F32, name="acc%d" % i, tag="bank")
+            for g in range(2):
+                nc.tensor.matmul_mx(
+                    out=acc[:],
+                    lhsT=k_codes[i][:, g * P : (g + 1) * P].bitcast(FP8X4),
+                    lhsT_scale=k_scales[i][:, g * P : (g + 1) * P],
+                    rhs=s_codes[g][:].bitcast(FP8X4),
+                    rhs_scale=s_scales[g][:],
+                    start=(g == 0),
+                    stop=(g == 1),
+                )
+            accs[i] = acc
+
+        def add_bias(i):
+            vp = keep.tile([P, OUTF], F32, name="vp%d" % i, tag="vp%d" % i)
+            nc.vector.tensor_tensor(out=vp[:], in0=accs[i][:], in1=b1[:], op=ALU.add)
+            vps[i] = vp
+            neg = keep.tile([P, OUTF], F32, name="neg%d" % i, tag="neg%d" % i)
+            negs[i] = neg
+
+        def clamp_vector(i):
+            nc.vector.tensor_scalar(
+                out=negs[i][:], in0=vps[i][:], scalar1=-1.0, scalar2=1.0, op0=ALU.min, op1=ALU.add
+            )
+
+        def exponent(i):
+            on_scalar = i in MIN_ON_SCALAR
+            if on_scalar:
+                nc.scalar.activation(out=negs[i][:], in_=vps[i][:], func=ACT.Relu, scale=-1.0, bias=-1.0)
+            ex = keep.tile([P, OUTF], F32, name="ex%d" % i, tag="ex%d" % i)
+            for cols in pieces(i):
+                nc.scalar.activation(
+                    out=ex[:, cols], in_=negs[i][:, cols], func=ACT.Exp, scale=(-1.0 if on_scalar else 1.0)
+                )
+            exps[i] = ex
+
+        def finish(i):
+            res = keep.tile([P, OUTF], F32, name="res%d" % i, tag="res%d" % i)
+            for cols in pieces(i):
+                nc.vector.scalar_tensor_tensor(
+                    out=res[:, cols], in0=vps[i][:, cols], scalar=-1.0, in1=exps[i][:, cols], op0=ALU.max, op1=ALU.add
+                )
+                nc.sync.dma_start(out=out[i * P : (i + 1) * P, cols], in_=res[:, cols])
+
+        multiply(0)
+        a_quant(1)
+        nc.vector.tensor_scalar_add(out=b1[:], in0=bank_b[:], scalar1=-1.0)
+        add_bias(0)
+        a_quant(2)
+        clamp_vector(0)
+        for j in range(9):
+            if j + 1 < 8:
+                multiply(j + 1)
+            if j + AHEAD + 1 < 8:
+                banks_a[j + AHEAD + 1] = a_turn(j + AHEAD + 1)
+            if j + AHEAD < 8:
+                a_square(j + AHEAD, banks_a[j + AHEAD])
+            if j < 8:
+                exponent(j)
+            if AHEAD <= j + AHEAD - 1 < 8:
+                a_quant(j + AHEAD - 1)
+            if j + 1 < 8:
+                add_bias(j + 1)
+            if j >= 1:
+                finish(j - 1)
+            if j + 1 < 8 and (j + 1) not in MIN_ON_SCALAR:
+                clamp_vector(j + 1)

@@ -19,7 +19,9 @@ FEAT = 512
 OUTF = 512
 MANUAL = True
 AHEAD = 3
-NWARM = 6
+NWARM = 5
+NWARM_LATE = 3
+XC_ON_VECTOR = (1,)
 MIN_ON_SCALAR = (5, 6)
 SPLIT_TILES = (7,)
 SC_ON_VECTOR = (1, 3)
@@ -72,7 +74,10 @@ def tile_netgraphconvolution_kernel(tc, x, adj, weight, bias, out):
         HALF = OUTF // 2
         for c in range(2):
             cols = slice(c * HALF, (c + 1) * HALF)
-            nc.vector.tensor_copy(out=w_grp[:, cols, :], in_=w_raw[:, :, cols].rearrange("p j o -> p o j"))
+            nc.vector.tensor_copy(
+                out=w_grp[:, cols, :].rearrange("p (c i) j -> p c j i", i=4),
+                in_=w_raw[:, :, cols].rearrange("p j (c i) -> p c j i", i=4),
+            )
         for c in range(2):
             cols = slice(c * HALF, (c + 1) * HALF)
             nc.vector.quantize_mx(
@@ -93,7 +98,8 @@ def tile_netgraphconvolution_kernel(tc, x, adj, weight, bias, out):
                     c0 = e * 256 + s * P
                     nc.tensor.transpose(out=bank[:, c0 : c0 + P], in_=words[:, e:256:2], identity=ident[:])
             grp = keep.tile([P, 1024], BF16, name="x_grp%d" % u, tag="x_grp%d" % u, align_bytes=64)
-            nc.scalar.copy(
+            copy = nc.vector.tensor_copy if u in XC_ON_VECTOR else nc.scalar.copy
+            copy(
                 out=grp[:].bitcast(F32).rearrange("p (q e) -> p q e", e=2),
                 in_=bank[:].rearrange("p (e q) -> p q e", e=2),
             )
@@ -180,7 +186,20 @@ def tile_netgraphconvolution_kernel(tc, x, adj, weight, bias, out):
             scales = keep.tile([P, OUTF], U8, name="s_scales%d" % g, tag="s_scales%d" % g, align_bytes=64)
             for c in range(2):
                 cols = slice(c * HALF, (c + 1) * HALF)
-                nc.vector.tensor_copy(out=grp[:, cols, :], in_=s_raw[g][:, :, cols].rearrange("p t o -> p o t"))
+                nc.vector.tensor_copy(
+                    out=grp[:, cols, :].rearrange("p (c i) t -> p c t i", i=4),
+                    in_=s_raw[g][:, :, cols].rearrange("p t (c i) -> p c t i", i=4),
+                )
+                if g == 1 and c == 0:
+                    bank_w2 = psum.tile([P, OUTF], F32, name="bank_w2", tag="bank")
+                    for n in range(NWARM_LATE):
+                        nc.tensor.matmul(
+                            out=bank_w2[:],
+                            lhsT=ones[:],
+                            rhs=grp[:, 0:P, :].rearrange("p o t -> p (o t)"),
+                            start=True,
+                            stop=True,
+                        )
             if g == 1:
                 a_quant(0)
             for c in range(2):

from contextlib import ExitStack

import concourse.mybir as mybir
from concourse.masks import make_identity

FLOPS = 2 * 1024 * 512 * 512 + 2 * 1024 * 1024 * 512

F32 = mybir.dt.float32
BF16 = mybir.dt.bfloat16
U32 = mybir.dt.uint32
U8 = mybir.dt.uint8
FP8X4 = mybir.dt.float8_e4m3fn_x4
ALU = mybir.AluOpType
ACT = mybir.ActivationFunctionType

P = 128
NODES = 1024
FEAT = 512
OUTF = 512
MANUAL = True
AHEAD = 3
NWARM = 5
NWARM_LATE = 3
XC_ON_VECTOR = (1,)
MIN_ON_SCALAR = (5, 6)
SPLIT_TILES = (7,)
SC_ON_VECTOR = (1, 3)
BANK_DT = F32


def tile_netgraphconvolution_kernel(tc, x, adj, weight, bias, out):
    nc = tc.nc
    with ExitStack() as ctx:
        keep = ctx.enter_context(tc.tile_pool(name="keep", bufs=1))
        psum = ctx.enter_context(tc.psum_pool(name="psum", bufs=8))
        if MANUAL:
            ctx.enter_context(tc.manual_schedule())

        bias_row = keep.tile([P, OUTF], BF16, name="bias_row", tag="bias_row")
        ones = keep.tile([P, P], BF16, name="ones", tag="ones")
        warm = keep.tile([P, 8], F32, name="warm", tag="warm")
        zeros = keep.tile([P, OUTF], BF16, name="zeros", tag="zeros")
        nc.vector.memset(warm[:], 0.0)
        nc.vector.memset(ones[:], 1.0)
        nc.vector.memset(zeros[:], 0.0)
        nc.vector.memset(bias_row[:], 0.0)
        nc.scalar.activation(out=warm[:, 4:8], in_=warm[:, 0:4], func=ACT.Exp)
        nc.scalar.dma_start(out=bias_row[0:1, :], in_=bias.rearrange("(a o) -> a o", a=1))

        w_raw = keep.tile([P, 4, OUTF], BF16, name="w_raw", tag="w_raw")
        nc.sync.dma_start(out=w_raw[:], in_=weight.rearrange("(p j) o -> p j o", j=4))
        x_view = x.rearrange("(u m s) f -> u m s f", m=P, s=4)
        x_raw = []
        for u in range(4):
            t = keep.tile([P, 2, FEAT], BF16, name="x_raw%d" % u, tag="x_raw%d" % u)
            g, h = divmod(u, 2)
            nc.sync.dma_start(out=t[:], in_=x_view[g, :, 2 * h : 2 * h + 2, :])
            x_raw.append(t)
        a_raw = []
        for i in range(8):
            t = keep.tile([P, NODES], BF16, name="a_raw%d" % i, tag="a_raw%d" % i)
            nc.sync.dma_start(out=t[:], in_=adj[i * P : (i + 1) * P, :])
            a_raw.append(t)

        ident = keep.tile([P, P], F32, name="ident", tag="ident")
        make_identity(nc, ident[:])
        bank_w = psum.tile([P, OUTF], F32, name="bank_w", tag="bank")
        for n in range(NWARM):
            nc.tensor.matmul(out=bank_w[:], lhsT=ones[:], rhs=zeros[:], start=True, stop=True)

        w_grp = keep.tile([P, OUTF, 4], BF16, name="w_grp", tag="w_grp", align_bytes=64)
        w_codes = keep.tile([P, OUTF], U32, name="w_codes", tag="w_codes", align_bytes=64)
        w_scales = keep.tile([P, OUTF], U8, name="w_scales", tag="w_scales", align_bytes=64)
        HALF = OUTF // 2
        for c in range(2):
            cols = slice(c * HALF, (c + 1) * HALF)
            nc.vector.tensor_copy(
                out=w_grp[:, cols, :].rearrange("p (c i) j -> p c j i", i=4),
                in_=w_raw[:, :, cols].rearrange("p j (c i) -> p c j i", i=4),
            )
        for c in range(2):
            cols = slice(c * HALF, (c + 1) * HALF)
            nc.vector.quantize_mx(
                out=w_codes[:, cols].bitcast(FP8X4),
                scales=w_scales[:, cols],
                in_=w_grp[:, cols, :].rearrange("p o j -> p (o j)"),
            )

        x_codes = []
        x_scales = []
        x_grp = []

        def x_turn(u):
            bank = psum.tile([P, 512], F32, name="bank_x%d" % u, tag="bank")
            for s in range(2):
                words = x_raw[u][:, s, :].bitcast(F32)
                for e in range(2):
                    c0 = e * 256 + s * P
                    nc.tensor.transpose(out=bank[:, c0 : c0 + P], in_=words[:, e:256:2], identity=ident[:])
            grp = keep.tile([P, 1024], BF16, name="x_grp%d" % u, tag="x_grp%d" % u, align_bytes=64)
            copy = nc.vector.tensor_copy if u in XC_ON_VECTOR else nc.scalar.copy
            copy(
                out=grp[:].bitcast(F32).rearrange("p (q e) -> p q e", e=2),
                in_=bank[:].rearrange("p (e q) -> p q e", e=2),
            )
            x_grp.append(grp)

        def x_quant(u):
            codes = keep.tile([P, 256], U32, name="x_codes%d" % u, tag="x_codes%d" % u, align_bytes=64)
            scales = keep.tile([P, 256], U8, name="x_scales%d" % u, tag="x_scales%d" % u, align_bytes=64)
            nc.vector.quantize_mx(out=codes[:].bitcast(FP8X4), scales=scales[:], in_=x_grp[u][:])
            x_codes.append(codes)
            x_scales.append(scales)

        for u in range(4):
            x_turn(u)
            x_quant(u)


        k_grp = {}
        k_codes = {}
        k_scales = {}

        def a_turn(i):
            bank = psum.tile([P, 512], F32, name="bank_a%d" % i, tag="bank")
            words = a_raw[i][:].bitcast(F32)
            for g in range(2):
                for e in range(2):
                    c0 = e * 256 + g * P
                    nc.tensor.transpose(
                        out=bank[:, c0 : c0 + P], in_=words[:, 256 * g + e : 256 * (g + 1) : 2], identity=ident[:]
                    )
            return bank

        def a_square(i, bank):
            grp = keep.tile([P, 1024], BF16, name="k_grp%d" % i, tag="k_grp%d" % i, align_bytes=64)
            nc.scalar.activation(
                out=grp[:].rearrange("p (q e c) -> p q e c", e=2, c=2),
                in_=bank[:].bitcast(BF16).rearrange("p (e q c) -> p q e c", e=2, c=2),
                func=ACT.Square,
            )
            k_grp[i] = grp

        def a_quant(i):
            codes = keep.tile([P, 256], U32, name="k_codes%d" % i, tag="k_codes%d" % i, align_bytes=64)
            scales = keep.tile([P, 256], U8, name="k_scales%d" % i, tag="k_scales%d" % i, align_bytes=64)
            nc.vector.quantize_mx(out=codes[:].bitcast(FP8X4), scales=scales[:], in_=k_grp[i][:])
            k_codes[i] = codes
            k_scales[i] = scales

        s_raw = []
        for g in range(2):
            s_raw_g = keep.tile([P, 4, OUTF], BF16, name="s_raw%d" % g, tag="s_raw%d" % g)
            s_raw.append(s_raw_g)
        for k in range(8):
            u, s = divmod(k, 2)
            g, t = divmod(k, 4)
            bank = psum.tile([P, OUTF], BANK_DT, name="bank_s%d" % k, tag="bank")
            nc.tensor.matmul_mx(
                out=bank[:],
                lhsT=x_codes[u][:, s * P : (s + 1) * P].bitcast(FP8X4),
                lhsT_scale=x_scales[u][:, s * P : (s + 1) * P],
                rhs=w_codes[:].bitcast(FP8X4),
                rhs_scale=w_scales[:],
                start=True,
                stop=True,
            )
            if k in SC_ON_VECTOR:
                nc.vector.tensor_copy(out=s_raw[g][:, t, :], in_=bank[:])
            else:
                nc.scalar.copy(out=s_raw[g][:, t, :], in_=bank[:])

        banks_a = {}
        for i in range(AHEAD):
            a_square(i, a_turn(i))
        banks_a[AHEAD] = a_turn(AHEAD)
        bank_b = psum.tile([P, OUTF], F32, name="bank_b", tag="bank")
        nc.tensor.matmul(out=bank_b[:], lhsT=ones[:], rhs=bias_row[:], start=True, stop=True)
        b1 = keep.tile([P, OUTF], F32, name="b1", tag="b1")

        s_codes = []
        s_scales = []
        for g in range(2):
            grp = keep.tile([P, OUTF, 4], BF16, name="s_grp%d" % g, tag="s_grp%d" % g, align_bytes=64)
            codes = keep.tile([P, OUTF], U32, name="s_codes%d" % g, tag="s_codes%d" % g, align_bytes=64)
            scales = keep.tile([P, OUTF], U8, name="s_scales%d" % g, tag="s_scales%d" % g, align_bytes=64)
            for c in range(2):
                cols = slice(c * HALF, (c + 1) * HALF)
                nc.vector.tensor_copy(
                    out=grp[:, cols, :].rearrange("p (c i) t -> p c t i", i=4),
                    in_=s_raw[g][:, :, cols].rearrange("p t (c i) -> p c t i", i=4),
                )
                if g == 1 and c == 0:
                    bank_w2 = psum.tile([P, OUTF], F32, name="bank_w2", tag="bank")
                    for n in range(NWARM_LATE):
                        nc.tensor.matmul(
                            out=bank_w2[:],
                            lhsT=ones[:],
                            rhs=grp[:, 0:P, :].rearrange("p o t -> p (o t)"),
                            start=True,
                            stop=True,
                        )
            if g == 1:
                a_quant(0)
            for c in range(2):
                cols = slice(c * HALF, (c + 1) * HALF)
                nc.vector.quantize_mx(
                    out=codes[:, cols].bitcast(FP8X4),
                    scales=scales[:, cols],
                    in_=grp[:, cols, :].rearrange("p o t -> p (o t)"),
                )
            s_codes.append(codes)
            s_scales.append(scales)

        accs = {}
        vps = {}
        negs = {}
        exps = {}

        def pieces(i):
            if i in SPLIT_TILES:
                return [slice(0, HALF), slice(HALF, OUTF)]
            return [slice(0, OUTF)]

        def multiply(i):
            acc = psum.tile([P, OUTF], F32, name="acc%d" % i, tag="bank")
            for g in range(2):
                nc.tensor.matmul_mx(
                    out=acc[:],
                    lhsT=k_codes[i][:, g * P : (g + 1) * P].bitcast(FP8X4),
                    lhsT_scale=k_scales[i][:, g * P : (g + 1) * P],
                    rhs=s_codes[g][:].bitcast(FP8X4),
                    rhs_scale=s_scales[g][:],
                    start=(g == 0),
                    stop=(g == 1),
                )
            accs[i] = acc

        def add_bias(i):
            vp = keep.tile([P, OUTF], F32, name="vp%d" % i, tag="vp%d" % i)
            nc.vector.tensor_tensor(out=vp[:], in0=accs[i][:], in1=b1[:], op=ALU.add)
            vps[i] = vp
            neg = keep.tile([P, OUTF], F32, name="neg%d" % i, tag="neg%d" % i)
            negs[i] = neg

        def clamp_vector(i):
            nc.vector.tensor_scalar(
                out=negs[i][:], in0=vps[i][:], scalar1=-1.0, scalar2=1.0, op0=ALU.min, op1=ALU.add
            )

        def exponent(i):
            on_scalar = i in MIN_ON_SCALAR
            if on_scalar:
                nc.scalar.activation(out=negs[i][:], in_=vps[i][:], func=ACT.Relu, scale=-1.0, bias=-1.0)
            ex = keep.tile([P, OUTF], F32, name="ex%d" % i, tag="ex%d" % i)
            for cols in pieces(i):
                nc.scalar.activation(
                    out=ex[:, cols], in_=negs[i][:, cols], func=ACT.Exp, scale=(-1.0 if on_scalar else 1.0)
                )
            exps[i] = ex

        def finish(i):
            res = keep.tile([P, OUTF], F32, name="res%d" % i, tag="res%d" % i)
            for cols in pieces(i):
                nc.vector.scalar_tensor_tensor(
                    out=res[:, cols], in0=vps[i][:, cols], scalar=-1.0, in1=exps[i][:, cols], op0=ALU.max, op1=ALU.add
                )
                nc.sync.dma_start(out=out[i * P : (i + 1) * P, cols], in_=res[:, cols])

        multiply(0)
        a_quant(1)
        nc.vector.tensor_scalar_add(out=b1[:], in0=bank_b[:], scalar1=-1.0)
        add_bias(0)
        a_quant(2)
        clamp_vector(0)
        for j in range(9):
            if j + 1 < 8:
                multiply(j + 1)
            if j + AHEAD + 1 < 8:
                banks_a[j + AHEAD + 1] = a_turn(j + AHEAD + 1)
            if j + AHEAD < 8:
                a_square(j + AHEAD, banks_a[j + AHEAD])
            if j < 8:
                exponent(j)
            if AHEAD <= j + AHEAD - 1 < 8:
                a_quant(j + AHEAD - 1)
            if j + 1 < 8:
                add_bias(j + 1)
            if j >= 1:
                finish(j - 1)
            if j + 1 < 8 and (j + 1) not in MIN_ON_SCALAR:
                clamp_vector(j + 1)
